import numpy as np
import ml_dtypes


def mxq(x, axis, fmt="e4m3"):
    dtype, down = {"e4m3": (ml_dtypes.float8_e4m3fn, 7), "e5m2": (ml_dtypes.float8_e5m2, 14)}[fmt]
    v = np.moveaxis(np.asarray(x, np.float32).astype(ml_dtypes.bfloat16).astype(np.float64), axis, -1)
    blocks = v.reshape(v.shape[:-1] + (-1, 32))
    amax = np.abs(blocks).max(-1, keepdims=True)
    byte = np.maximum(np.where(amax > 0, np.frexp(amax)[1] - 1 + 127, 0) - down, 1)
    scale = np.exp2(byte - 127.0)
    codes = (blocks / scale).astype(np.float32).astype(dtype).astype(np.float64)
    return np.moveaxis((codes * scale).reshape(v.shape), -1, axis)


WIDE = False


def mx_kscale(k):
    if not WIDE:
        return np.ones(k)
    levels = np.array([10, -10, 5, -5, 0])
    a = np.random.permutation(np.resize(levels, k // 512 * 4)).reshape(k // 512, 4)
    idx = np.arange(k)
    return np.exp2(a[idx // 512, idx % 128 // 32])


BF16 = ml_dtypes.bfloat16


def bf(x):
    return np.asarray(x, np.float32).astype(BF16)


def f64(x):
    return np.asarray(x).astype(np.float64)


E2M1 = np.array([0.0, 0.5, 1.0, 1.5, 2.0, 3.0, 4.0, 6.0, -0.0, -0.5, -1.0, -1.5, -2.0, -3.0, -4.0, -6.0])


def pack_weight(w, fmt):
    k, n = w.shape
    w = f64(bf(w)).reshape(k // 32, 32, n)
    amax = np.abs(w).max(1)
    if fmt == "e4m3":
        byte = np.frexp(amax)[1] - 1 + 127 - 7
    else:
        mant, ex = np.frexp(amax / 6.0)
        byte = np.where(mant > 0.5, ex, ex - 1) + 127
    byte = np.clip(np.where(amax > 0, byte, 1), 1, 254)
    scaled = (w * np.exp2(127.0 - byte)[:, None, :]).reshape(k, n).astype(np.float32)
    by_word = np.ascontiguousarray(scaled.reshape(k // 512, 128, 4, n).transpose(0, 1, 3, 2))
    if fmt == "e4m3":
        words = by_word.astype(ml_dtypes.float8_e4m3fn).view(np.uint8)
    else:
        c = by_word.astype(ml_dtypes.float4_e2m1fn).view(np.uint8) & 0xF
        words = c[..., 0::2] | (c[..., 1::2] << 4)
    return np.ascontiguousarray(words), np.ascontiguousarray(byte.astype(np.uint8).reshape(k // 512, 16, n))


def unpack_weight(words, scales, fmt):
    g, p, n, _ = words.shape
    if fmt == "e4m3":
        vals = np.ascontiguousarray(words).view(ml_dtypes.float8_e4m3fn).astype(np.float64)
    else:
        nib = np.empty((g, p, n, 4), np.uint8)
        nib[..., 0::2] = words & 0xF
        nib[..., 1::2] = words >> 4
        vals = E2M1[nib]
    vals = vals * np.repeat(np.exp2(scales.astype(np.float64) - 127.0), 8, axis=1)[..., None]
    return vals.transpose(0, 1, 3, 2).reshape(g * 512, n)

def pack4(w):
    words, scales = pack_weight(w, "e2m1")
    return words.reshape(words.shape[0], 128, -1), scales


def unpack4(words, scales):
    return unpack_weight(words.reshape(words.shape[0], 128, -1, 2), scales, "e2m1")


B, HH, WW, C, NH, DIM = 4, 32, 32, 1024, 8, 32
N = HH * WW
HD = NH * DIM
F = 4 * HD
BN_EPS = 1e-5
WS = 0.02
GQK = np.sqrt(2.8) / DIM ** 0.25
GV = 4.0


def heads(t):
    return t.reshape(B, N, NH, DIM).transpose(0, 2, 1, 3)


def setup_inputs():
    s = mx_kscale(C)
    x = np.random.standard_normal((B, HH, WW, C)) + 0.5 * np.random.standard_normal(C)
    gain = np.concatenate([np.full(2 * HD, GQK), np.full(2 * HD, GV)])
    inputs = bf(x * s)
    words, scales = pack4(np.random.standard_normal((C, F)) * WS / np.sqrt(C) / s[:, None])
    return {"inputs": inputs,
            "w_qkv_words": words,
            "w_qkv_scales": scales,
            "bn_scale": bf(np.random.standard_normal(F) * gain)}


def reference(inputs, w_qkv_words, w_qkv_scales, bn_scale):
    x = mxq(f64(inputs).reshape(B * N, C), 1, "e4m3") @ unpack4(w_qkv_words, w_qkv_scales)
    mean = x.mean(axis=0)
    var = x.var(axis=0)
    x = (x - mean) / np.sqrt(var + BN_EPS) * f64(bn_scale)
    q, k, v1, v2 = (heads(t) for t in np.split(x.reshape(B, N, F), 4, axis=-1))
    v = np.concatenate((v1, v2), axis=-1)
    return np.ascontiguousarray(q), np.ascontiguousarray(k), v

@@ -1,0 +1,261 @@
+from contextlib import ExitStack
+
+import concourse.masks as masks
+import concourse.mybir as mybir
+
+F32 = mybir.dt.float32
+BF16 = mybir.dt.bfloat16
+I32 = mybir.dt.int32
+U32 = mybir.dt.uint32
+U8 = mybir.dt.uint8
+FP8X4 = mybir.dt.float8_e4m3fn_x4
+FP4X4 = mybir.dt.float4_e2m1fn_x4
+ACT = mybir.ActivationFunctionType
+ALU = mybir.AluOpType
+
+P = 128
+MAPS, ROWS, COLS, CHANNELS = 4, 32, 32, 1024
+PIXELS = MAPS * ROWS * COLS
+COLUMNS = 1024
+PACK = 4
+K_PASS = P * PACK
+PASSES = CHANNELS // K_PASS
+WORDS_PER_PASS = K_PASS // 2
+N_TILE = 512
+CHUNK_COLS = N_TILE // P
+CHUNKS = PIXELS // N_TILE
+M_TILE = 128
+TILES = COLUMNS // M_TILE
+HEAD = 32
+HEADS_PER_TILE = M_TILE // HEAD
+PIECE = 1024
+PIECES_PER_TILE = PIXELS // PIECE
+BN_EPS = 1e-5
+FLIP_LAG = 2 * PIECES_PER_TILE + 1
+
+FLOPS = 2 * PIXELS * CHANNELS * COLUMNS
+
+
+def tile_levitattention_pa_t_kernel(
+    tc, inputs, w_qkv_words, w_qkv_scales, bn_scale, out_0, out_1, out_2
+):
+    nc = tc.nc
+    with ExitStack() as ctx:
+        keep = ctx.enter_context(tc.tile_pool(name="keep", bufs=1))
+        x_pool = ctx.enter_context(tc.tile_pool(name="x", bufs=3))
+        grouped_pool = ctx.enter_context(tc.tile_pool(name="grouped", bufs=2 * PASSES))
+        flipped_pool = ctx.enter_context(tc.tile_pool(name="flipped", bufs=3))
+        psum = ctx.enter_context(tc.psum_pool(name="psum", bufs=8))
+
+        x_rows = inputs.rearrange("b i j c -> (b i) j c")
+        x_chunks = []
+
+        def load_x(s):
+            x_sb = x_pool.tile([P, CHUNK_COLS, CHANNELS], BF16, tag="x")
+            nc.sync.dma_start(
+                out=x_sb[:], in_=x_rows[:, s * CHUNK_COLS : (s + 1) * CHUNK_COLS, :]
+            )
+            x_chunks.append(x_sb)
+
+        load_x(0)
+
+        w_scale_planes = keep.tile([P, PASSES, COLUMNS], U8, align_bytes=64)
+        nc.vector.memset(w_scale_planes[:].bitcast(I32), 0)
+        for quadrant in range(4):
+            nc.sync.dma_start(
+                out=w_scale_planes[32 * quadrant : 32 * quadrant + 4].bitcast(I32),
+                in_=w_qkv_scales[:, 4 * quadrant : 4 * quadrant + 4, :]
+                .rearrange("g r n -> r g n")
+                .bitcast(I32),
+            )
+        w_words = keep.tile([P, PASSES, 2 * COLUMNS], U8, align_bytes=64)
+        nc.sync.dma_start(
+            out=w_words[:].bitcast(I32),
+            in_=w_qkv_words.rearrange("g p n -> p g n").bitcast(I32),
+        )
+        gain_rows = keep.tile([P, P], BF16)
+        nc.vector.memset(gain_rows[:], 0.0)
+        nc.sync.dma_start(
+            out=gain_rows[0:TILES, :], in_=bn_scale.rearrange("(m p) -> m p", p=P)
+        )
+        load_x(1)
+        load_x(2)
+
+        identity_f32 = keep.tile([P, P], F32)
+        masks.make_identity(nc, identity_f32[:])
+        identity_bf16 = keep.tile([P, P], BF16)
+        masks.make_identity(nc, identity_bf16[:])
+        eps = keep.tile([P, 1], F32)
+        nc.vector.memset(eps[:], BN_EPS)
+        table_warmer = keep.tile([P, 1], F32)
+        nc.scalar.activation(out=table_warmer[:], in_=eps[:], func=ACT.Sqrt)
+
+        gain_bank = psum.tile([P, P], BF16, tag="bank")
+        nc.tensor.transpose(gain_bank[:], gain_rows[:], identity_bf16[:])
+        gain = keep.tile([P, TILES], F32)
+        nc.vector.tensor_copy(out=gain[:], in_=gain_bank[:, 0:TILES])
+
+        x_codes = keep.tile([P, PASSES, PIXELS], U32, align_bytes=64)
+        x_scale_planes = keep.tile([P, PASSES, PIXELS], U8, align_bytes=64)
+        grouped_tiles = {}
+
+        def transpose_chunk(s):
+            words = x_chunks[s][:].rearrange("p j c -> p (j c)").bitcast(F32)
+            for g in range(PASSES):
+                grouped = grouped_pool.tile([P, N_TILE, PACK], BF16, tag="grouped", align_bytes=64)
+                grouped_words = (
+                    grouped[:]
+                    .rearrange("p n t -> p (n t)")
+                    .bitcast(F32)
+                    .rearrange("p (n u) -> p n u", u=2)
+                )
+                for half in range(2):
+                    bank = psum.tile([P, 2, N_TILE // 2], F32, tag="bank")
+                    for u in range(2):
+                        for jj in range(2):
+                            first = (2 * half + jj) * (CHANNELS // 2) + g * WORDS_PER_PASS + u
+                            nc.tensor.transpose(
+                                bank[:, u, jj * P : (jj + 1) * P],
+                                words[:, first : first + WORDS_PER_PASS - 1 : 2],
+                                identity_f32[:],
+                            )
+                    nc.scalar.copy(
+                        out=grouped_words[:, half * (N_TILE // 2) : (half + 1) * (N_TILE // 2), :],
+                        in_=bank[:].rearrange("p u n -> p n u"),
+                    )
+                grouped_tiles[(s, g)] = grouped
+
+        def quantise_chunk(s):
+            pixels = slice(s * N_TILE, (s + 1) * N_TILE)
+            for g in range(PASSES):
+                nc.vector.quantize_mx(
+                    out=x_codes[:, g, pixels].bitcast(FP8X4),
+                    scales=x_scale_planes[:, g, pixels],
+                    in_=grouped_tiles[(s, g)][:].rearrange("p n t -> p (n t)"),
+                )
+
+        blocks = (
+            (out_2, 0, (4, 6)),
+            (out_2, 1, (5, 7)),
+            (out_0, 0, (0,)),
+            (out_0, 1, (1,)),
+            (out_1, 0, (2,)),
+            (out_1, 1, (3,)),
+        )
+        column_tiles = []
+        pieces = []
+        for number, (out, head_group, members) in enumerate(blocks):
+            parts = len(members)
+            y = keep.tile(
+                [P, MAPS, COLS, parts, ROWS], F32, tag="y%d" % number, align_bytes=64
+            )
+            for h, m in enumerate(members):
+                column_tiles.append((m, y, h))
+            y_flat = y[:].rearrange("p b j h i -> p (b j h i)")
+            heads = slice(head_group * HEADS_PER_TILE, (head_group + 1) * HEADS_PER_TILE)
+            rows_of_out = out[:, heads, :, :].rearrange("b a (i j) f -> (a i) b (j f)", j=COLS)
+            for n in range(parts * PIECES_PER_TILE):
+                b, part_of_map = divmod(n, parts)
+                pieces.append(
+                    (
+                        y_flat[:, n * PIECE : (n + 1) * PIECE],
+                        rows_of_out[:, b, part_of_map * PIECE : (part_of_map + 1) * PIECE],
+                    )
+                )
+
+        stats = keep.tile([P, TILES, CHUNKS, 6], F32)
+        mean_var = keep.tile([P, TILES, 2], F32)
+        minus_mean = keep.tile([P, TILES], F32)
+        deviation = keep.tile([P, TILES], F32)
+        inverse_deviation = keep.tile([P, TILES], F32)
+        scale = keep.tile([P, TILES], F32)
+
+        def multiply(r, s):
+            m, y, h = column_tiles[r]
+            pixels = slice(s * N_TILE, (s + 1) * N_TILE)
+            bank = psum.tile([P, N_TILE], F32, tag="bank")
+            for g in range(PASSES):
+                nc.tensor.matmul_mx(
+                    out=bank[:],
+                    lhsT=w_words[:, g, 2 * m * M_TILE : 2 * (m + 1) * M_TILE].bitcast(FP4X4),
+                    lhsT_scale=w_scale_planes[:, g, m * M_TILE : (m + 1) * M_TILE],
+                    rhs=x_codes[:, g, pixels].bitcast(FP8X4),
+                    rhs_scale=x_scale_planes[:, g, pixels],
+                    start=(g == 0),
+                    stop=(g == PASSES - 1),
+                )
+            y_chunk = y[:, :, s * CHUNK_COLS : (s + 1) * CHUNK_COLS, h, :]
+            nc.scalar.copy(
+                out=y_chunk.rearrange("p b j i -> p j b i"),
+                in_=bank[:].rearrange("p (j b i) -> p j b i", j=CHUNK_COLS, b=MAPS),
+            )
+            nc.vector.bn_stats(out=stats[:, r, s, :], in_=y_chunk)
+
+        def begin_scale(r):
+            nc.vector.bn_aggr(
+                out=mean_var[:, r, :], in_=stats[:, r, :, :].rearrange("p s k -> p (s k)")
+            )
+            nc.vector.tensor_scalar_mul(
+                out=minus_mean[:, r : r + 1], in0=mean_var[:, r, 0:1], scalar1=-1.0
+            )
+            nc.scalar.activation(
+                out=deviation[:, r : r + 1],
+                in_=mean_var[:, r, 1:2],
+                func=ACT.Sqrt,
+                bias=eps[:, 0:1],
+                scale=1.0,
+            )
+
+        def finish_scale(r):
+            m = column_tiles[r][0]
+            nc.vector.reciprocal(
+                out=inverse_deviation[:, r : r + 1], in_=deviation[:, r : r + 1]
+            )
+            nc.vector.tensor_mul(
+                out=scale[:, r : r + 1],
+                in0=inverse_deviation[:, r : r + 1],
+                in1=gain[:, m : m + 1],
+            )
+
+        def normalise(r):
+            y, h = column_tiles[r][1], column_tiles[r][2]
+            for b in range(MAPS):
+                nc.gpsimd.tensor_scalar(
+                    out=y[:, b, :, h, :],
+                    in0=y[:, b, :, h, :],
+                    scalar1=minus_mean[:, r : r + 1],
+                    scalar2=scale[:, r : r + 1],
+                    op0=ALU.add,
+                    op1=ALU.mult,
+                )
+
+        def flip_and_store(n):
+            source, destination = pieces[n]
+            flipped = flipped_pool.tile([P, PIECE], F32, tag="flipped", align_bytes=64)
+            nc.vector.transpose(out=flipped[:], in_=source)
+            nc.sync.dma_start(out=destination, in_=flipped[:])
+
+        transpose_chunk(0)
+        for s in range(CHUNKS):
+            if s + 1 < CHUNKS:
+                transpose_chunk(s + 1)
+            if s + 3 < CHUNKS:
+                load_x(s + 3)
+            quantise_chunk(s)
+            multiply(0, s)
+        begin_scale(0)
+
+        last_round = (len(pieces) - 1 + FLIP_LAG) // PIECES_PER_TILE
+        for r in range(1, last_round + 1):
+            for s in range(CHUNKS):
+                if r < TILES:
+                    multiply(r, s)
+                if s == 0 and r - 1 < TILES:
+                    finish_scale(r - 1)
+                    normalise(r - 1)
+                if s % 2 == 1:
+                    n = PIECES_PER_TILE * r + s // 2 - FLIP_LAG
+                    if 0 <= n < len(pieces):
+                        flip_and_store(n)
+            if r < TILES:
+                begin_scale(r)

@@ -31,7 +31,6 @@ HEADS_PER_TILE = M_TILE // HEAD
 PIECE = 1024
 PIECES_PER_TILE = PIXELS // PIECE
 BN_EPS = 1e-5
-FLIP_LAG = 2 * PIECES_PER_TILE + 1
 
 FLOPS = 2 * PIXELS * CHANNELS * COLUMNS
 
@@ -50,14 +49,17 @@ def tile_levitattention_pa_t_kernel(
         x_rows = inputs.rearrange("b i j c -> (b i) j c")
         x_chunks = []
 
-        def load_x(s):
+        def load_x(s, cuts):
             x_sb = x_pool.tile([P, CHUNK_COLS, CHANNELS], BF16, tag="x")
-            nc.sync.dma_start(
-                out=x_sb[:], in_=x_rows[:, s * CHUNK_COLS : (s + 1) * CHUNK_COLS, :]
-            )
+            width = CHUNK_COLS // cuts
+            for c in range(cuts):
+                nc.sync.dma_start(
+                    out=x_sb[:, c * width : (c + 1) * width, :],
+                    in_=x_rows[:, s * CHUNK_COLS + c * width : s * CHUNK_COLS + (c + 1) * width, :],
+                )
             x_chunks.append(x_sb)
 
-        load_x(0)
+        load_x(0, 2)
 
         w_scale_planes = keep.tile([P, PASSES, COLUMNS], U8, align_bytes=64)
         nc.vector.memset(w_scale_planes[:].bitcast(I32), 0)
@@ -78,8 +80,8 @@ def tile_levitattention_pa_t_kernel(
         nc.sync.dma_start(
             out=gain_rows[0:TILES, :], in_=bn_scale.rearrange("(m p) -> m p", p=P)
         )
-        load_x(1)
-        load_x(2)
+        load_x(1, 1)
+        load_x(2, 1)
 
         identity_f32 = keep.tile([P, P], F32)
         masks.make_identity(nc, identity_f32[:])
@@ -89,11 +91,6 @@ def tile_levitattention_pa_t_kernel(
         nc.vector.memset(eps[:], BN_EPS)
         table_warmer = keep.tile([P, 1], F32)
         nc.scalar.activation(out=table_warmer[:], in_=eps[:], func=ACT.Sqrt)
-
-        gain_bank = psum.tile([P, P], BF16, tag="bank")
-        nc.tensor.transpose(gain_bank[:], gain_rows[:], identity_bf16[:])
-        gain = keep.tile([P, TILES], F32)
-        nc.vector.tensor_copy(out=gain[:], in_=gain_bank[:, 0:TILES])
 
         x_codes = keep.tile([P, PASSES, PIXELS], U32, align_bytes=64)
         x_scale_planes = keep.tile([P, PASSES, PIXELS], U8, align_bytes=64)
@@ -165,10 +162,18 @@ def tile_levitattention_pa_t_kernel(
 
         stats = keep.tile([P, TILES, CHUNKS, 6], F32)
         mean_var = keep.tile([P, TILES, 2], F32)
-        minus_mean = keep.tile([P, TILES], F32)
+        minus_mean_vector = keep.tile([P, TILES], F32)
+        bank_sums = keep.tile([P, TILES, CHUNKS], F32)
+        map_squares = keep.tile([P, TILES, MAPS], F32)
+        totals = keep.tile([P, TILES, 2], F32)
+        minus_mean_scalar = keep.tile([P, TILES], F32)
+        discarded = keep.tile([P, PIECE], BF16)
         deviation = keep.tile([P, TILES], F32)
         inverse_deviation = keep.tile([P, TILES], F32)
         scale = keep.tile([P, TILES], F32)
+
+        def statistics_on_scalar(r):
+            return r > 0 and r % 2 == 0
 
         def multiply(r, s):
             m, y, h = column_tiles[r]
@@ -185,26 +190,59 @@ def tile_levitattention_pa_t_kernel(
                     stop=(g == PASSES - 1),
                 )
             y_chunk = y[:, :, s * CHUNK_COLS : (s + 1) * CHUNK_COLS, h, :]
-            nc.scalar.copy(
-                out=y_chunk.rearrange("p b j i -> p j b i"),
-                in_=bank[:].rearrange("p (j b i) -> p j b i", j=CHUNK_COLS, b=MAPS),
-            )
-            nc.vector.bn_stats(out=stats[:, r, s, :], in_=y_chunk)
+            if statistics_on_scalar(r):
+                nc.scalar.activation(
+                    out=y_chunk.rearrange("p b j i -> p j b i"),
+                    in_=bank[:].rearrange("p (j b i) -> p j b i", j=CHUNK_COLS, b=MAPS),
+                    func=ACT.Identity,
+                    accum_out=bank_sums[:, r, s : s + 1],
+                )
+            else:
+                nc.scalar.copy(
+                    out=y_chunk.rearrange("p b j i -> p j b i"),
+                    in_=bank[:].rearrange("p (j b i) -> p j b i", j=CHUNK_COLS, b=MAPS),
+                )
+                nc.vector.bn_stats(out=stats[:, r, s, :], in_=y_chunk)
 
         def begin_scale(r):
-            nc.vector.bn_aggr(
-                out=mean_var[:, r, :], in_=stats[:, r, :, :].rearrange("p s k -> p (s k)")
-            )
-            nc.vector.tensor_scalar_mul(
-                out=minus_mean[:, r : r + 1], in0=mean_var[:, r, 0:1], scalar1=-1.0
-            )
-            nc.scalar.activation(
-                out=deviation[:, r : r + 1],
-                in_=mean_var[:, r, 1:2],
-                func=ACT.Sqrt,
-                bias=eps[:, 0:1],
-                scale=1.0,
-            )
+            one = slice(r, r + 1)
+            if statistics_on_scalar(r):
+                y, h = column_tiles[r][1], column_tiles[r][2]
+                nc.scalar.activation(
+                    out=discarded[:, 0:CHUNKS], in_=bank_sums[:, r, :], func=ACT.Identity,
+                    accum_out=totals[:, r, 0:1],
+                )
+                nc.scalar.mul(
+                    out=minus_mean_scalar[:, one], in_=totals[:, r, 0:1], mul=-1.0 / PIXELS
+                )
+                for b in range(MAPS):
+                    nc.scalar.activation(
+                        out=discarded[:].rearrange("p (j i) -> p j i", i=ROWS),
+                        in_=y[:, b, :, h, :],
+                        func=ACT.Square,
+                        bias=minus_mean_scalar[:, one],
+                        scale=1.0,
+                        accum_out=map_squares[:, r, b : b + 1],
+                    )
+                nc.scalar.activation(
+                    out=discarded[:, 0:MAPS], in_=map_squares[:, r, :], func=ACT.Identity,
+                    accum_out=totals[:, r, 1:2],
+                )
+                nc.scalar.activation(
+                    out=deviation[:, one], in_=totals[:, r, 1:2], func=ACT.Sqrt,
+                    bias=eps[:, 0:1], scale=1.0 / PIXELS,
+                )
+            else:
+                nc.vector.bn_aggr(
+                    out=mean_var[:, r, :], in_=stats[:, r, :, :].rearrange("p s k -> p (s k)")
+                )
+                nc.vector.tensor_scalar_mul(
+                    out=minus_mean_vector[:, one], in0=mean_var[:, r, 0:1], scalar1=-1.0
+                )
+                nc.scalar.activation(
+                    out=deviation[:, one], in_=mean_var[:, r, 1:2], func=ACT.Sqrt,
+                    bias=eps[:, 0:1], scale=1.0,
+                )
 
         def finish_scale(r):
             m = column_tiles[r][0]
@@ -219,6 +257,7 @@ def tile_levitattention_pa_t_kernel(
 
         def normalise(r):
             y, h = column_tiles[r][1], column_tiles[r][2]
+            minus_mean = minus_mean_scalar if statistics_on_scalar(r) else minus_mean_vector
             for b in range(MAPS):
                 nc.gpsimd.tensor_scalar(
                     out=y[:, b, :, h, :],
@@ -240,22 +279,22 @@ def tile_levitattention_pa_t_kernel(
             if s + 1 < CHUNKS:
                 transpose_chunk(s + 1)
             if s + 3 < CHUNKS:
-                load_x(s + 3)
+                load_x(s + 3, 1)
             quantise_chunk(s)
             multiply(0, s)
-        begin_scale(0)
 
-        last_round = (len(pieces) - 1 + FLIP_LAG) // PIECES_PER_TILE
-        for r in range(1, last_round + 1):
-            for s in range(CHUNKS):
-                if r < TILES:
+        gain_bank = psum.tile([P, P], BF16, tag="bank")
+        nc.tensor.transpose(gain_bank[:], gain_rows[:], identity_bf16[:])
+        gain = keep.tile([P, TILES], F32)
+        nc.vector.tensor_copy(out=gain[:], in_=gain_bank[:, 0:TILES])
+
+        for r in range(TILES):
+            if r > 0:
+                for s in range(CHUNKS):
                     multiply(r, s)
-                if s == 0 and r - 1 < TILES:
-                    finish_scale(r - 1)
-                    normalise(r - 1)
-                if s % 2 == 1:
-                    n = PIECES_PER_TILE * r + s // 2 - FLIP_LAG
-                    if 0 <= n < len(pieces):
-                        flip_and_store(n)
-            if r < TILES:
-                begin_scale(r)
+            begin_scale(r)
+            finish_scale(r)
+            normalise(r)
+
+        for n in range(len(pieces)):
+            flip_and_store(n)

@@ -31,6 +31,7 @@ HEADS_PER_TILE = M_TILE // HEAD
 PIECE = 1024
 PIECES_PER_TILE = PIXELS // PIECE
 BN_EPS = 1e-5
+EARLY_TILES = 2
 
 FLOPS = 2 * PIXELS * CHANNELS * COLUMNS
 
@@ -281,7 +282,8 @@ def tile_levitattention_pa_t_kernel(
             if s + 3 < CHUNKS:
                 load_x(s + 3, 1)
             quantise_chunk(s)
-            multiply(0, s)
+            for r in range(EARLY_TILES):
+                multiply(r, s)
 
         gain_bank = psum.tile([P, P], BF16, tag="bank")
         nc.tensor.transpose(gain_bank[:], gain_rows[:], identity_bf16[:])
@@ -289,7 +291,7 @@ def tile_levitattention_pa_t_kernel(
         nc.vector.tensor_copy(out=gain[:], in_=gain_bank[:, 0:TILES])
 
         for r in range(TILES):
-            if r > 0:
+            if r >= EARLY_TILES:
                 for s in range(CHUNKS):
                     multiply(r, s)
             begin_scale(r)

@@ -31,7 +31,7 @@ HEADS_PER_TILE = M_TILE // HEAD
 PIECE = 1024
 PIECES_PER_TILE = PIXELS // PIECE
 BN_EPS = 1e-5
-EARLY_TILES = 2
+FLIPPED_BUFS = 8
 
 FLOPS = 2 * PIXELS * CHANNELS * COLUMNS
 
@@ -42,248 +42,243 @@ def tile_levitattention_pa_t_kernel(
     nc = tc.nc
     with ExitStack() as ctx:
         keep = ctx.enter_context(tc.tile_pool(name="keep", bufs=1))
-        x_pool = ctx.enter_context(tc.tile_pool(name="x", bufs=3))
-        grouped_pool = ctx.enter_context(tc.tile_pool(name="grouped", bufs=2 * PASSES))
-        flipped_pool = ctx.enter_context(tc.tile_pool(name="flipped", bufs=3))
         psum = ctx.enter_context(tc.psum_pool(name="psum", bufs=8))
+        with ExitStack() as arrival:
+            x_pool = arrival.enter_context(tc.tile_pool(name="x", bufs=3))
+            grouped_pool = arrival.enter_context(tc.tile_pool(name="grouped", bufs=2 * PASSES))
 
-        x_rows = inputs.rearrange("b i j c -> (b i) j c")
-        x_chunks = []
+            x_rows = inputs.rearrange("b i j c -> (b i) j c")
+            x_chunks = []
 
-        def load_x(s, cuts):
-            x_sb = x_pool.tile([P, CHUNK_COLS, CHANNELS], BF16, tag="x")
-            width = CHUNK_COLS // cuts
-            for c in range(cuts):
+            def load_x(s, cuts):
+                x_sb = x_pool.tile([P, CHUNK_COLS, CHANNELS], BF16, tag="x")
+                width = CHUNK_COLS // cuts
+                for c in range(cuts):
+                    nc.sync.dma_start(
+                        out=x_sb[:, c * width : (c + 1) * width, :],
+                        in_=x_rows[:, s * CHUNK_COLS + c * width : s * CHUNK_COLS + (c + 1) * width, :],
+                    )
+                x_chunks.append(x_sb)
+
+            load_x(0, 2)
+
+            w_scale_planes = keep.tile([P, PASSES, COLUMNS], U8, align_bytes=64)
+            nc.vector.memset(w_scale_planes[:].bitcast(I32), 0)
+            for quadrant in range(4):
                 nc.sync.dma_start(
-                    out=x_sb[:, c * width : (c + 1) * width, :],
-                    in_=x_rows[:, s * CHUNK_COLS + c * width : s * CHUNK_COLS + (c + 1) * width, :],
+                    out=w_scale_planes[32 * quadrant : 32 * quadrant + 4].bitcast(I32),
+                    in_=w_qkv_scales[:, 4 * quadrant : 4 * quadrant + 4, :]
+                    .rearrange("g r n -> r g n")
+                    .bitcast(I32),
                 )
-            x_chunks.append(x_sb)
-
-        load_x(0, 2)
-
-        w_scale_planes = keep.tile([P, PASSES, COLUMNS], U8, align_bytes=64)
-        nc.vector.memset(w_scale_planes[:].bitcast(I32), 0)
-        for quadrant in range(4):
+            w_words = keep.tile([P, PASSES, 2 * COLUMNS], U8, align_bytes=64)
             nc.sync.dma_start(
-                out=w_scale_planes[32 * quadrant : 32 * quadrant + 4].bitcast(I32),
-                in_=w_qkv_scales[:, 4 * quadrant : 4 * quadrant + 4, :]
-                .rearrange("g r n -> r g n")
-                .bitcast(I32),
+                out=w_words[:].bitcast(I32),
+                in_=w_qkv_words.rearrange("g p n -> p g n").bitcast(I32),
             )
-        w_words = keep.tile([P, PASSES, 2 * COLUMNS], U8, align_bytes=64)
-        nc.sync.dma_start(
-            out=w_words[:].bitcast(I32),
-            in_=w_qkv_words.rearrange("g p n -> p g n").bitcast(I32),
-        )
-        gain_rows = keep.tile([P, P], BF16)
-        nc.vector.memset(gain_rows[:], 0.0)
-        nc.sync.dma_start(
-            out=gain_rows[0:TILES, :], in_=bn_scale.rearrange("(m p) -> m p", p=P)
-        )
-        load_x(1, 1)
-        load_x(2, 1)
-
-        identity_f32 = keep.tile([P, P], F32)
-        masks.make_identity(nc, identity_f32[:])
-        identity_bf16 = keep.tile([P, P], BF16)
-        masks.make_identity(nc, identity_bf16[:])
-        eps = keep.tile([P, 1], F32)
-        nc.vector.memset(eps[:], BN_EPS)
-        table_warmer = keep.tile([P, 1], F32)
-        nc.scalar.activation(out=table_warmer[:], in_=eps[:], func=ACT.Sqrt)
-
-        x_codes = keep.tile([P, PASSES, PIXELS], U32, align_bytes=64)
-        x_scale_planes = keep.tile([P, PASSES, PIXELS], U8, align_bytes=64)
-        grouped_tiles = {}
-
-        def transpose_chunk(s):
-            words = x_chunks[s][:].rearrange("p j c -> p (j c)").bitcast(F32)
-            for g in range(PASSES):
-                grouped = grouped_pool.tile([P, N_TILE, PACK], BF16, tag="grouped", align_bytes=64)
-                grouped_words = (
-                    grouped[:]
-                    .rearrange("p n t -> p (n t)")
-                    .bitcast(F32)
-                    .rearrange("p (n u) -> p n u", u=2)
-                )
-                for half in range(2):
-                    bank = psum.tile([P, 2, N_TILE // 2], F32, tag="bank")
-                    for u in range(2):
-                        for jj in range(2):
-                            first = (2 * half + jj) * (CHANNELS // 2) + g * WORDS_PER_PASS + u
-                            nc.tensor.transpose(
-                                bank[:, u, jj * P : (jj + 1) * P],
-                                words[:, first : first + WORDS_PER_PASS - 1 : 2],
-                                identity_f32[:],
-                            )
-                    nc.scalar.copy(
-                        out=grouped_words[:, half * (N_TILE // 2) : (half + 1) * (N_TILE // 2), :],
-                        in_=bank[:].rearrange("p u n -> p n u"),
-                    )
-                grouped_tiles[(s, g)] = grouped
-
-        def quantise_chunk(s):
-            pixels = slice(s * N_TILE, (s + 1) * N_TILE)
-            for g in range(PASSES):
-                nc.vector.quantize_mx(
-                    out=x_codes[:, g, pixels].bitcast(FP8X4),
-                    scales=x_scale_planes[:, g, pixels],
-                    in_=grouped_tiles[(s, g)][:].rearrange("p n t -> p (n t)"),
-                )
-
-        blocks = (
-            (out_2, 0, (4, 6)),
-            (out_2, 1, (5, 7)),
-            (out_0, 0, (0,)),
-            (out_0, 1, (1,)),
-            (out_1, 0, (2,)),
-            (out_1, 1, (3,)),
-        )
-        column_tiles = []
-        pieces = []
-        for number, (out, head_group, members) in enumerate(blocks):
-            parts = len(members)
-            y = keep.tile(
-                [P, MAPS, COLS, parts, ROWS], F32, tag="y%d" % number, align_bytes=64
+            gain_rows = keep.tile([P, P], BF16)
+            nc.vector.memset(gain_rows[:], 0.0)
+            nc.sync.dma_start(
+                out=gain_rows[0:TILES, :], in_=bn_scale.rearrange("(m p) -> m p", p=P)
             )
-            for h, m in enumerate(members):
-                column_tiles.append((m, y, h))
-            y_flat = y[:].rearrange("p b j h i -> p (b j h i)")
-            heads = slice(head_group * HEADS_PER_TILE, (head_group + 1) * HEADS_PER_TILE)
-            rows_of_out = out[:, heads, :, :].rearrange("b a (i j) f -> (a i) b (j f)", j=COLS)
-            for n in range(parts * PIECES_PER_TILE):
-                b, part_of_map = divmod(n, parts)
-                pieces.append(
-                    (
-                        y_flat[:, n * PIECE : (n + 1) * PIECE],
-                        rows_of_out[:, b, part_of_map * PIECE : (part_of_map + 1) * PIECE],
+            load_x(1, 1)
+            load_x(2, 1)
+
+            identity_f32 = keep.tile([P, P], F32)
+            masks.make_identity(nc, identity_f32[:])
+            identity_bf16 = keep.tile([P, P], BF16)
+            masks.make_identity(nc, identity_bf16[:])
+            eps = keep.tile([P, 1], F32)
+            nc.vector.memset(eps[:], BN_EPS)
+            table_warmer = keep.tile([P, 1], F32)
+            nc.scalar.activation(out=table_warmer[:], in_=eps[:], func=ACT.Sqrt)
+
+            x_codes = keep.tile([P, PASSES, PIXELS], U32, align_bytes=64)
+            x_scale_planes = keep.tile([P, PASSES, PIXELS], U8, align_bytes=64)
+            grouped_tiles = {}
+
+            def transpose_chunk(s):
+                words = x_chunks[s][:].rearrange("p j c -> p (j c)").bitcast(F32)
+                for g in range(PASSES):
+                    grouped = grouped_pool.tile([P, N_TILE, PACK], BF16, tag="grouped", align_bytes=64)
+                    grouped_words = (
+                        grouped[:]
+                        .rearrange("p n t -> p (n t)")
+                        .bitcast(F32)
+                        .rearrange("p (n u) -> p n u", u=2)
                     )
-                )
+                    for half in range(2):
+                        bank = psum.tile([P, 2, N_TILE // 2], F32, tag="bank")
+                        for u in range(2):
+                            for jj in range(2):
+                                first = (2 * half + jj) * (CHANNELS // 2) + g * WORDS_PER_PASS + u
+                                nc.tensor.transpose(
+                                    bank[:, u, jj * P : (jj + 1) * P],
+                                    words[:, first : first + WORDS_PER_PASS - 1 : 2],
+                                    identity_f32[:],
+                                )
+                        nc.scalar.copy(
+                            out=grouped_words[:, half * (N_TILE // 2) : (half + 1) * (N_TILE // 2), :],
+                            in_=bank[:].rearrange("p u n -> p n u"),
+                        )
+                    grouped_tiles[(s, g)] = grouped
 
-        stats = keep.tile([P, TILES, CHUNKS, 6], F32)
-        mean_var = keep.tile([P, TILES, 2], F32)
-        minus_mean_vector = keep.tile([P, TILES], F32)
-        bank_sums = keep.tile([P, TILES, CHUNKS], F32)
-        map_squares = keep.tile([P, TILES, MAPS], F32)
-        totals = keep.tile([P, TILES, 2], F32)
-        minus_mean_scalar = keep.tile([P, TILES], F32)
-        discarded = keep.tile([P, PIECE], BF16)
-        deviation = keep.tile([P, TILES], F32)
-        inverse_deviation = keep.tile([P, TILES], F32)
-        scale = keep.tile([P, TILES], F32)
+            def quantise_chunk(s):
+                pixels = slice(s * N_TILE, (s + 1) * N_TILE)
+                for g in range(PASSES):
+                    nc.vector.quantize_mx(
+                        out=x_codes[:, g, pixels].bitcast(FP8X4),
+                        scales=x_scale_planes[:, g, pixels],
+                        in_=grouped_tiles[(s, g)][:].rearrange("p n t -> p (n t)"),
+                    )
 
-        def statistics_on_scalar(r):
-            return r > 0 and r % 2 == 0
+            blocks = (
+                (out_2, 0, (4, 6)),
+                (out_2, 1, (5, 7)),
+                (out_0, 0, (0,)),
+                (out_0, 1, (1,)),
+                (out_1, 0, (2,)),
+                (out_1, 1, (3,)),
+            )
+            column_tiles = []
+            pieces = []
+            for number, (out, head_group, members) in enumerate(blocks):
+                parts = len(members)
+                y = keep.tile(
+                    [P, MAPS, COLS, parts, ROWS], F32, tag="y%d" % number, align_bytes=64
+                )
+                for h, m in enumerate(members):
+                    column_tiles.append((m, y, h))
+                y_flat = y[:].rearrange("p b j h i -> p (b j h i)")
+                heads = slice(head_group * HEADS_PER_TILE, (head_group + 1) * HEADS_PER_TILE)
+                rows_of_out = out[:, heads, :, :].rearrange("b a (i j) f -> (a i) b (j f)", j=COLS)
+                for n in range(parts * PIECES_PER_TILE):
+                    b, part_of_map = divmod(n, parts)
+                    pieces.append(
+                        (
+                            y_flat[:, n * PIECE : (n + 1) * PIECE],
+                            rows_of_out[:, b, part_of_map * PIECE : (part_of_map + 1) * PIECE],
+                        )
+                    )
 
-        def multiply(r, s):
-            m, y, h = column_tiles[r]
-            pixels = slice(s * N_TILE, (s + 1) * N_TILE)
-            bank = psum.tile([P, N_TILE], F32, tag="bank")
-            for g in range(PASSES):
-                nc.tensor.matmul_mx(
-                    out=bank[:],
-                    lhsT=w_words[:, g, 2 * m * M_TILE : 2 * (m + 1) * M_TILE].bitcast(FP4X4),
-                    lhsT_scale=w_scale_planes[:, g, m * M_TILE : (m + 1) * M_TILE],
-                    rhs=x_codes[:, g, pixels].bitcast(FP8X4),
-                    rhs_scale=x_scale_planes[:, g, pixels],
-                    start=(g == 0),
-                    stop=(g == PASSES - 1),
-                )
-            y_chunk = y[:, :, s * CHUNK_COLS : (s + 1) * CHUNK_COLS, h, :]
-            if statistics_on_scalar(r):
-                nc.scalar.activation(
-                    out=y_chunk.rearrange("p b j i -> p j b i"),
-                    in_=bank[:].rearrange("p (j b i) -> p j b i", j=CHUNK_COLS, b=MAPS),
-                    func=ACT.Identity,
-                    accum_out=bank_sums[:, r, s : s + 1],
-                )
-            else:
-                nc.scalar.copy(
-                    out=y_chunk.rearrange("p b j i -> p j b i"),
-                    in_=bank[:].rearrange("p (j b i) -> p j b i", j=CHUNK_COLS, b=MAPS),
-                )
-                nc.vector.bn_stats(out=stats[:, r, s, :], in_=y_chunk)
+            stats = keep.tile([P, TILES, CHUNKS, 6], F32)
+            mean_var = keep.tile([P, TILES, 2], F32)
+            minus_mean_vector = keep.tile([P, TILES], F32)
+            bank_sums = keep.tile([P, TILES, CHUNKS], F32)
+            totals = keep.tile([P, TILES, 2], F32)
+            minus_mean_scalar = keep.tile([P, TILES], F32)
+            discarded = keep.tile([P, PIXELS], BF16)
+            deviation = keep.tile([P, TILES], F32)
+            inverse_deviation = keep.tile([P, TILES], F32)
+            scale = keep.tile([P, TILES], F32)
 
-        def begin_scale(r):
-            one = slice(r, r + 1)
-            if statistics_on_scalar(r):
-                y, h = column_tiles[r][1], column_tiles[r][2]
-                nc.scalar.activation(
-                    out=discarded[:, 0:CHUNKS], in_=bank_sums[:, r, :], func=ACT.Identity,
-                    accum_out=totals[:, r, 0:1],
-                )
-                nc.scalar.mul(
-                    out=minus_mean_scalar[:, one], in_=totals[:, r, 0:1], mul=-1.0 / PIXELS
-                )
-                for b in range(MAPS):
+            def statistics_on_scalar(r):
+                return r > 1 and r % 2 == 1
+
+            def multiply(r, s):
+                m, y, h = column_tiles[r]
+                pixels = slice(s * N_TILE, (s + 1) * N_TILE)
+                bank = psum.tile([P, N_TILE], F32, tag="bank")
+                for g in range(PASSES):
+                    nc.tensor.matmul_mx(
+                        out=bank[:],
+                        lhsT=w_words[:, g, 2 * m * M_TILE : 2 * (m + 1) * M_TILE].bitcast(FP4X4),
+                        lhsT_scale=w_scale_planes[:, g, m * M_TILE : (m + 1) * M_TILE],
+                        rhs=x_codes[:, g, pixels].bitcast(FP8X4),
+                        rhs_scale=x_scale_planes[:, g, pixels],
+                        start=(g == 0),
+                        stop=(g == PASSES - 1),
+                    )
+                y_chunk = y[:, :, s * CHUNK_COLS : (s + 1) * CHUNK_COLS, h, :]
+                if statistics_on_scalar(r):
                     nc.scalar.activation(
-                        out=discarded[:].rearrange("p (j i) -> p j i", i=ROWS),
-                        in_=y[:, b, :, h, :],
+                        out=y_chunk.rearrange("p b j i -> p j b i"),
+                        in_=bank[:].rearrange("p (j b i) -> p j b i", j=CHUNK_COLS, b=MAPS),
+                        func=ACT.Identity,
+                        accum_out=bank_sums[:, r, s : s + 1],
+                    )
+                else:
+                    nc.scalar.copy(
+                        out=y_chunk.rearrange("p b j i -> p j b i"),
+                        in_=bank[:].rearrange("p (j b i) -> p j b i", j=CHUNK_COLS, b=MAPS),
+                    )
+                    nc.vector.bn_stats(out=stats[:, r, s, :], in_=y_chunk)
+
+            def begin_scale(r):
+                one = slice(r, r + 1)
+                if statistics_on_scalar(r):
+                    y, h = column_tiles[r][1], column_tiles[r][2]
+                    nc.scalar.activation(
+                        out=discarded[:, 0:CHUNKS], in_=bank_sums[:, r, :], func=ACT.Identity,
+                        accum_out=totals[:, r, 0:1],
+                    )
+                    nc.scalar.mul(
+                        out=minus_mean_scalar[:, one], in_=totals[:, r, 0:1], mul=-1.0 / PIXELS
+                    )
+                    nc.scalar.activation(
+                        out=discarded[:].rearrange("p (b j i) -> p b j i", b=MAPS, i=ROWS),
+                        in_=y[:, :, :, h, :],
                         func=ACT.Square,
                         bias=minus_mean_scalar[:, one],
                         scale=1.0,
-                        accum_out=map_squares[:, r, b : b + 1],
+                        accum_out=totals[:, r, 1:2],
                     )
-                nc.scalar.activation(
-                    out=discarded[:, 0:MAPS], in_=map_squares[:, r, :], func=ACT.Identity,
-                    accum_out=totals[:, r, 1:2],
+                    nc.scalar.activation(
+                        out=deviation[:, one], in_=totals[:, r, 1:2], func=ACT.Sqrt,
+                        bias=eps[:, 0:1], scale=1.0 / PIXELS,
+                    )
+                else:
+                    nc.vector.bn_aggr(
+                        out=mean_var[:, r, :], in_=stats[:, r, :, :].rearrange("p s k -> p (s k)")
+                    )
+                    nc.vector.tensor_scalar_mul(
+                        out=minus_mean_vector[:, one], in0=mean_var[:, r, 0:1], scalar1=-1.0
+                    )
+                    nc.scalar.activation(
+                        out=deviation[:, one], in_=mean_var[:, r, 1:2], func=ACT.Sqrt,
+                        bias=eps[:, 0:1], scale=1.0,
+                    )
+
+            def finish_scale(r):
+                m = column_tiles[r][0]
+                nc.vector.reciprocal(
+                    out=inverse_deviation[:, r : r + 1], in_=deviation[:, r : r + 1]
                 )
-                nc.scalar.activation(
-                    out=deviation[:, one], in_=totals[:, r, 1:2], func=ACT.Sqrt,
-                    bias=eps[:, 0:1], scale=1.0 / PIXELS,
-                )
-            else:
-                nc.vector.bn_aggr(
-                    out=mean_var[:, r, :], in_=stats[:, r, :, :].rearrange("p s k -> p (s k)")
-                )
-                nc.vector.tensor_scalar_mul(
-                    out=minus_mean_vector[:, one], in0=mean_var[:, r, 0:1], scalar1=-1.0
-                )
-                nc.scalar.activation(
-                    out=deviation[:, one], in_=mean_var[:, r, 1:2], func=ACT.Sqrt,
-                    bias=eps[:, 0:1], scale=1.0,
+                nc.vector.tensor_mul(
+                    out=scale[:, r : r + 1],
+                    in0=inverse_deviation[:, r : r + 1],
+                    in1=gain[:, m : m + 1],
                 )
 
-        def finish_scale(r):
-            m = column_tiles[r][0]
-            nc.vector.reciprocal(
-                out=inverse_deviation[:, r : r + 1], in_=deviation[:, r : r + 1]
-            )
-            nc.vector.tensor_mul(
-                out=scale[:, r : r + 1],
-                in0=inverse_deviation[:, r : r + 1],
-                in1=gain[:, m : m + 1],
-            )
+            def normalise(r):
+                y, h = column_tiles[r][1], column_tiles[r][2]
+                minus_mean = minus_mean_scalar if statistics_on_scalar(r) else minus_mean_vector
+                for b in range(MAPS):
+                    nc.gpsimd.tensor_scalar(
+                        out=y[:, b, :, h, :],
+                        in0=y[:, b, :, h, :],
+                        scalar1=minus_mean[:, r : r + 1],
+                        scalar2=scale[:, r : r + 1],
+                        op0=ALU.add,
+                        op1=ALU.mult,
+                    )
 
-        def normalise(r):
-            y, h = column_tiles[r][1], column_tiles[r][2]
-            minus_mean = minus_mean_scalar if statistics_on_scalar(r) else minus_mean_vector
-            for b in range(MAPS):
-                nc.gpsimd.tensor_scalar(
-                    out=y[:, b, :, h, :],
-                    in0=y[:, b, :, h, :],
-                    scalar1=minus_mean[:, r : r + 1],
-                    scalar2=scale[:, r : r + 1],
-                    op0=ALU.add,
-                    op1=ALU.mult,
-                )
+            def flip_and_store(n):
+                source, destination = pieces[n]
+                flipped = flipped_pool.tile([P, PIECE], F32, tag="flipped", align_bytes=64)
+                nc.vector.transpose(out=flipped[:], in_=source)
+                nc.sync.dma_start(out=destination, in_=flipped[:])
 
-        def flip_and_store(n):
-            source, destination = pieces[n]
-            flipped = flipped_pool.tile([P, PIECE], F32, tag="flipped", align_bytes=64)
-            nc.vector.transpose(out=flipped[:], in_=source)
-            nc.sync.dma_start(out=destination, in_=flipped[:])
+            transpose_chunk(0)
+            for s in range(CHUNKS):
+                if s + 1 < CHUNKS:
+                    transpose_chunk(s + 1)
+                if s + 3 < CHUNKS:
+                    load_x(s + 3, 1)
+                quantise_chunk(s)
+                multiply(0, s)
 
-        transpose_chunk(0)
-        for s in range(CHUNKS):
-            if s + 1 < CHUNKS:
-                transpose_chunk(s + 1)
-            if s + 3 < CHUNKS:
-                load_x(s + 3, 1)
-            quantise_chunk(s)
-            for r in range(EARLY_TILES):
-                multiply(r, s)
+        flipped_pool = ctx.enter_context(tc.tile_pool(name="flipped", bufs=FLIPPED_BUFS))
 
         gain_bank = psum.tile([P, P], BF16, tag="bank")
         nc.tensor.transpose(gain_bank[:], gain_rows[:], identity_bf16[:])
@@ -291,7 +286,7 @@ def tile_levitattention_pa_t_kernel(
         nc.vector.tensor_copy(out=gain[:], in_=gain_bank[:, 0:TILES])
 
         for r in range(TILES):
-            if r >= EARLY_TILES:
+            if r > 0:
                 for s in range(CHUNKS):
                     multiply(r, s)
             begin_scale(r)

@@ -210,10 +210,7 @@ def tile_levitattention_pa_t_kernel(
                     y, h = column_tiles[r][1], column_tiles[r][2]
                     nc.scalar.activation(
                         out=discarded[:, 0:CHUNKS], in_=bank_sums[:, r, :], func=ACT.Identity,
-                        accum_out=totals[:, r, 0:1],
-                    )
-                    nc.scalar.mul(
-                        out=minus_mean_scalar[:, one], in_=totals[:, r, 0:1], mul=-1.0 / PIXELS
+                        scale=-1.0 / PIXELS, accum_out=minus_mean_scalar[:, one],
                     )
                     nc.scalar.activation(
                         out=discarded[:].rearrange("p (b j i) -> p b j i", b=MAPS, i=ROWS),
@@ -244,10 +241,10 @@ def tile_levitattention_pa_t_kernel(
                 nc.vector.reciprocal(
                     out=inverse_deviation[:, r : r + 1], in_=deviation[:, r : r + 1]
                 )
-                nc.vector.tensor_mul(
+                nc.vector.tensor_scalar_mul(
                     out=scale[:, r : r + 1],
                     in0=inverse_deviation[:, r : r + 1],
-                    in1=gain[:, m : m + 1],
+                    scalar1=gain[:, m : m + 1],
                 )
 
             def normalise(r):

@@ -60,7 +60,8 @@ def tile_levitattention_pa_t_kernel(
                     )
                 x_chunks.append(x_sb)
 
-            load_x(0, 2)
+            load_x(0, CHUNK_COLS)
+            load_x(1, 2)
 
             w_scale_planes = keep.tile([P, PASSES, COLUMNS], U8, align_bytes=64)
             nc.vector.memset(w_scale_planes[:].bitcast(I32), 0)
@@ -81,7 +82,6 @@ def tile_levitattention_pa_t_kernel(
             nc.sync.dma_start(
                 out=gain_rows[0:TILES, :], in_=bn_scale.rearrange("(m p) -> m p", p=P)
             )
-            load_x(1, 1)
             load_x(2, 1)
 
             identity_f32 = keep.tile([P, P], F32)
@@ -91,7 +91,7 @@ def tile_levitattention_pa_t_kernel(
             eps = keep.tile([P, 1], F32)
             nc.vector.memset(eps[:], BN_EPS)
             table_warmer = keep.tile([P, 1], F32)
-            nc.scalar.activation(out=table_warmer[:], in_=eps[:], func=ACT.Sqrt)
+            nc.scalar.activation(out=table_warmer[:], in_=eps[:], func=ACT.Abs_reciprocal_sqrt)
 
             x_codes = keep.tile([P, PASSES, PIXELS], U32, align_bytes=64)
             x_scale_planes = keep.tile([P, PASSES, PIXELS], U8, align_bytes=64)
@@ -117,7 +117,8 @@ def tile_levitattention_pa_t_kernel(
                                     words[:, first : first + WORDS_PER_PASS - 1 : 2],
                                     identity_f32[:],
                                 )
-                        nc.scalar.copy(
+                        copy_out = nc.vector.tensor_copy if (g == PASSES - 1 and half == 1) else nc.scalar.copy
+                        copy_out(
                             out=grouped_words[:, half * (N_TILE // 2) : (half + 1) * (N_TILE // 2), :],
                             in_=bank[:].rearrange("p u n -> p n u"),
                         )
@@ -168,9 +169,9 @@ def tile_levitattention_pa_t_kernel(
             totals = keep.tile([P, TILES, 2], F32)
             minus_mean_scalar = keep.tile([P, TILES], F32)
             discarded = keep.tile([P, PIXELS], BF16)
-            deviation = keep.tile([P, TILES], F32)
             inverse_deviation = keep.tile([P, TILES], F32)
             scale = keep.tile([P, TILES], F32)
+            last_shift = keep.tile([P, 1], F32)
 
             def statistics_on_scalar(r):
                 return r > 1 and r % 2 == 1
@@ -221,8 +222,8 @@ def tile_levitattention_pa_t_kernel(
                         accum_out=totals[:, r, 1:2],
                     )
                     nc.scalar.activation(
-                        out=deviation[:, one], in_=totals[:, r, 1:2], func=ACT.Sqrt,
-                        bias=eps[:, 0:1], scale=1.0 / PIXELS,
+                        out=inverse_deviation[:, one], in_=totals[:, r, 1:2],
+                        func=ACT.Abs_reciprocal_sqrt, bias=eps[:, 0:1], scale=1.0 / PIXELS,
                     )
                 else:
                     nc.vector.bn_aggr(
@@ -232,24 +233,31 @@ def tile_levitattention_pa_t_kernel(
                         out=minus_mean_vector[:, one], in0=mean_var[:, r, 0:1], scalar1=-1.0
                     )
                     nc.scalar.activation(
-                        out=deviation[:, one], in_=mean_var[:, r, 1:2], func=ACT.Sqrt,
-                        bias=eps[:, 0:1], scale=1.0,
+                        out=inverse_deviation[:, one], in_=mean_var[:, r, 1:2],
+                        func=ACT.Abs_reciprocal_sqrt, bias=eps[:, 0:1], scale=1.0,
                     )
 
             def finish_scale(r):
                 m = column_tiles[r][0]
-                nc.vector.reciprocal(
-                    out=inverse_deviation[:, r : r + 1], in_=deviation[:, r : r + 1]
-                )
-                nc.vector.tensor_scalar_mul(
-                    out=scale[:, r : r + 1],
-                    in0=inverse_deviation[:, r : r + 1],
-                    scalar1=gain[:, m : m + 1],
+                nc.scalar.activation(
+                    out=scale[:, r : r + 1], in_=inverse_deviation[:, r : r + 1], func=ACT.Identity,
+                    scale=gain[:, m : m + 1],
                 )
 
             def normalise(r):
                 y, h = column_tiles[r][1], column_tiles[r][2]
                 minus_mean = minus_mean_scalar if statistics_on_scalar(r) else minus_mean_vector
+                if r == TILES - 1:
+                    nc.scalar.activation(
+                        out=last_shift[:], in_=minus_mean[:, r : r + 1], func=ACT.Identity,
+                        scale=scale[:, r : r + 1],
+                    )
+                    for b in range(MAPS):
+                        nc.scalar.activation(
+                            out=y[:, b, :, h, :], in_=y[:, b, :, h, :], func=ACT.Identity,
+                            bias=last_shift[:, 0:1], scale=scale[:, r : r + 1],
+                        )
+                    return
                 for b in range(MAPS):
                     nc.gpsimd.tensor_scalar(
                         out=y[:, b, :, h, :],

@@ -45,12 +45,15 @@ def tile_levitattention_pa_t_kernel(
         psum = ctx.enter_context(tc.psum_pool(name="psum", bufs=8))
         with ExitStack() as arrival:
             x_pool = arrival.enter_context(tc.tile_pool(name="x", bufs=3))
+            sorted_pool = arrival.enter_context(tc.tile_pool(name="sorted", bufs=2))
             grouped_pool = arrival.enter_context(tc.tile_pool(name="grouped", bufs=2 * PASSES))
 
             x_rows = inputs.rearrange("b i j c -> (b i) j c")
             x_chunks = []
+            x_cuts = []
 
             def load_x(s, cuts):
+                x_cuts.append(cuts)
                 x_sb = x_pool.tile([P, CHUNK_COLS, CHANNELS], BF16, tag="x")
                 width = CHUNK_COLS // cuts
                 for c in range(cuts):
@@ -82,7 +85,7 @@ def tile_levitattention_pa_t_kernel(
             nc.sync.dma_start(
                 out=gain_rows[0:TILES, :], in_=bn_scale.rearrange("(m p) -> m p", p=P)
             )
-            load_x(2, 1)
+            load_x(2, 2)
 
             identity_f32 = keep.tile([P, P], F32)
             masks.make_identity(nc, identity_f32[:])
@@ -98,7 +101,19 @@ def tile_levitattention_pa_t_kernel(
             grouped_tiles = {}
 
             def transpose_chunk(s):
-                words = x_chunks[s][:].rearrange("p j c -> p (j c)").bitcast(F32)
+                words = (
+                    x_chunks[s][:]
+                    .rearrange("p j c -> p (j c)")
+                    .bitcast(F32)
+                    .rearrange("p (c q u) -> p c u q", q=P, u=2)
+                )
+                x_sorted = sorted_pool.tile([P, CHUNK_COLS * PASSES, 2, P], F32, tag="sorted")
+                width = CHUNK_COLS * PASSES // x_cuts[s]
+                for c in range(x_cuts[s]):
+                    nc.vector.tensor_copy(
+                        out=x_sorted[:, c * width : (c + 1) * width, :, :],
+                        in_=words[:, c * width : (c + 1) * width, :, :],
+                    )
                 for g in range(PASSES):
                     grouped = grouped_pool.tile([P, N_TILE, PACK], BF16, tag="grouped", align_bytes=64)
                     grouped_words = (
@@ -111,14 +126,12 @@ def tile_levitattention_pa_t_kernel(
                         bank = psum.tile([P, 2, N_TILE // 2], F32, tag="bank")
                         for u in range(2):
                             for jj in range(2):
-                                first = (2 * half + jj) * (CHANNELS // 2) + g * WORDS_PER_PASS + u
                                 nc.tensor.transpose(
                                     bank[:, u, jj * P : (jj + 1) * P],
-                                    words[:, first : first + WORDS_PER_PASS - 1 : 2],
+                                    x_sorted[:, (2 * half + jj) * PASSES + g, u, :],
                                     identity_f32[:],
                                 )
-                        copy_out = nc.vector.tensor_copy if (g == PASSES - 1 and half == 1) else nc.scalar.copy
-                        copy_out(
+                        nc.scalar.copy(
                             out=grouped_words[:, half * (N_TILE // 2) : (half + 1) * (N_TILE // 2), :],
                             in_=bank[:].rearrange("p u n -> p n u"),
                         )
@@ -168,7 +181,6 @@ def tile_levitattention_pa_t_kernel(
             bank_sums = keep.tile([P, TILES, CHUNKS], F32)
             totals = keep.tile([P, TILES, 2], F32)
             minus_mean_scalar = keep.tile([P, TILES], F32)
-            discarded = keep.tile([P, PIXELS], BF16)
             inverse_deviation = keep.tile([P, TILES], F32)
             scale = keep.tile([P, TILES], F32)
             last_shift = keep.tile([P, 1], F32)
@@ -279,11 +291,13 @@ def tile_levitattention_pa_t_kernel(
                 if s + 1 < CHUNKS:
                     transpose_chunk(s + 1)
                 if s + 3 < CHUNKS:
-                    load_x(s + 3, 1)
+                    load_x(s + 3, 2)
                 quantise_chunk(s)
                 multiply(0, s)
 
         flipped_pool = ctx.enter_context(tc.tile_pool(name="flipped", bufs=FLIPPED_BUFS))
+        late = ctx.enter_context(tc.tile_pool(name="late", bufs=1))
+        discarded = late.tile([P, PIXELS], BF16)
 
         gain_bank = psum.tile([P, P], BF16, tag="bank")
         nc.tensor.transpose(gain_bank[:], gain_rows[:], identity_bf16[:])

from contextlib import ExitStack

import concourse.masks as masks
import concourse.mybir as mybir

F32 = mybir.dt.float32
BF16 = mybir.dt.bfloat16
I32 = mybir.dt.int32
U32 = mybir.dt.uint32
U8 = mybir.dt.uint8
FP8X4 = mybir.dt.float8_e4m3fn_x4
FP4X4 = mybir.dt.float4_e2m1fn_x4
ACT = mybir.ActivationFunctionType
ALU = mybir.AluOpType

P = 128
MAPS, ROWS, COLS, CHANNELS = 4, 32, 32, 1024
PIXELS = MAPS * ROWS * COLS
COLUMNS = 1024
PACK = 4
K_PASS = P * PACK
PASSES = CHANNELS // K_PASS
WORDS_PER_PASS = K_PASS // 2
N_TILE = 512
CHUNK_COLS = N_TILE // P
CHUNKS = PIXELS // N_TILE
M_TILE = 128
TILES = COLUMNS // M_TILE
HEAD = 32
HEADS_PER_TILE = M_TILE // HEAD
PIECE = 1024
PIECES_PER_TILE = PIXELS // PIECE
BN_EPS = 1e-5
FLIPPED_BUFS = 8

FLOPS = 2 * PIXELS * CHANNELS * COLUMNS


def tile_levitattention_pa_t_kernel(
    tc, inputs, w_qkv_words, w_qkv_scales, bn_scale, out_0, out_1, out_2
):
    nc = tc.nc
    with ExitStack() as ctx:
        keep = ctx.enter_context(tc.tile_pool(name="keep", bufs=1))
        psum = ctx.enter_context(tc.psum_pool(name="psum", bufs=8))
        with ExitStack() as arrival:
            x_pool = arrival.enter_context(tc.tile_pool(name="x", bufs=3))
            sorted_pool = arrival.enter_context(tc.tile_pool(name="sorted", bufs=2))
            grouped_pool = arrival.enter_context(tc.tile_pool(name="grouped", bufs=2 * PASSES))

            x_rows = inputs.rearrange("b i j c -> (b i) j c")
            x_chunks = []
            x_cuts = []

            def load_x(s, cuts):
                x_cuts.append(cuts)
                x_sb = x_pool.tile([P, CHUNK_COLS, CHANNELS], BF16, tag="x")
                width = CHUNK_COLS // cuts
                for c in range(cuts):
                    nc.sync.dma_start(
                        out=x_sb[:, c * width : (c + 1) * width, :],
                        in_=x_rows[:, s * CHUNK_COLS + c * width : s * CHUNK_COLS + (c + 1) * width, :],
                    )
                x_chunks.append(x_sb)

            load_x(0, CHUNK_COLS)
            load_x(1, 2)

            w_scale_planes = keep.tile([P, PASSES, COLUMNS], U8, align_bytes=64)
            nc.vector.memset(w_scale_planes[:].bitcast(I32), 0)
            for quadrant in range(4):
                nc.sync.dma_start(
                    out=w_scale_planes[32 * quadrant : 32 * quadrant + 4].bitcast(I32),
                    in_=w_qkv_scales[:, 4 * quadrant : 4 * quadrant + 4, :]
                    .rearrange("g r n -> r g n")
                    .bitcast(I32),
                )
            w_words = keep.tile([P, PASSES, 2 * COLUMNS], U8, align_bytes=64)
            nc.sync.dma_start(
                out=w_words[:].bitcast(I32),
                in_=w_qkv_words.rearrange("g p n -> p g n").bitcast(I32),
            )
            gain_rows = keep.tile([P, P], BF16)
            nc.vector.memset(gain_rows[:], 0.0)
            nc.sync.dma_start(
                out=gain_rows[0:TILES, :], in_=bn_scale.rearrange("(m p) -> m p", p=P)
            )
            load_x(2, 2)

            identity_f32 = keep.tile([P, P], F32)
            masks.make_identity(nc, identity_f32[:])
            identity_bf16 = keep.tile([P, P], BF16)
            masks.make_identity(nc, identity_bf16[:])
            eps = keep.tile([P, 1], F32)
            nc.vector.memset(eps[:], BN_EPS)
            table_warmer = keep.tile([P, 1], F32)
            nc.scalar.activation(out=table_warmer[:], in_=eps[:], func=ACT.Abs_reciprocal_sqrt)

            x_codes = keep.tile([P, PASSES, PIXELS], U32, align_bytes=64)
            x_scale_planes = keep.tile([P, PASSES, PIXELS], U8, align_bytes=64)
            grouped_tiles = {}

            def transpose_chunk(s):
                words = (
                    x_chunks[s][:]
                    .rearrange("p j c -> p (j c)")
                    .bitcast(F32)
                    .rearrange("p (c q u) -> p c u q", q=P, u=2)
                )
                x_sorted = sorted_pool.tile([P, CHUNK_COLS * PASSES, 2, P], F32, tag="sorted")
                width = CHUNK_COLS * PASSES // x_cuts[s]
                for c in range(x_cuts[s]):
                    nc.vector.tensor_copy(
                        out=x_sorted[:, c * width : (c + 1) * width, :, :],
                        in_=words[:, c * width : (c + 1) * width, :, :],
                    )
                for g in range(PASSES):
                    grouped = grouped_pool.tile([P, N_TILE, PACK], BF16, tag="grouped", align_bytes=64)
                    grouped_words = (
                        grouped[:]
                        .rearrange("p n t -> p (n t)")
                        .bitcast(F32)
                        .rearrange("p (n u) -> p n u", u=2)
                    )
                    for half in range(2):
                        bank = psum.tile([P, 2, N_TILE // 2], F32, tag="bank")
                        for u in range(2):
                            for jj in range(2):
                                nc.tensor.transpose(
                                    bank[:, u, jj * P : (jj + 1) * P],
                                    x_sorted[:, (2 * half + jj) * PASSES + g, u, :],
                                    identity_f32[:],
                                )
                        nc.scalar.copy(
                            out=grouped_words[:, half * (N_TILE // 2) : (half + 1) * (N_TILE // 2), :],
                            in_=bank[:].rearrange("p u n -> p n u"),
                        )
                    grouped_tiles[(s, g)] = grouped

            def quantise_chunk(s):
                pixels = slice(s * N_TILE, (s + 1) * N_TILE)
                for g in range(PASSES):
                    nc.vector.quantize_mx(
                        out=x_codes[:, g, pixels].bitcast(FP8X4),
                        scales=x_scale_planes[:, g, pixels],
                        in_=grouped_tiles[(s, g)][:].rearrange("p n t -> p (n t)"),
                    )

            blocks = (
                (out_2, 0, (4, 6)),
                (out_2, 1, (5, 7)),
                (out_0, 0, (0,)),
                (out_0, 1, (1,)),
                (out_1, 0, (2,)),
                (out_1, 1, (3,)),
            )
            column_tiles = []
            pieces = []
            for number, (out, head_group, members) in enumerate(blocks):
                parts = len(members)
                y = keep.tile(
                    [P, MAPS, COLS, parts, ROWS], F32, tag="y%d" % number, align_bytes=64
                )
                for h, m in enumerate(members):
                    column_tiles.append((m, y, h))
                y_flat = y[:].rearrange("p b j h i -> p (b j h i)")
                heads = slice(head_group * HEADS_PER_TILE, (head_group + 1) * HEADS_PER_TILE)
                rows_of_out = out[:, heads, :, :].rearrange("b a (i j) f -> (a i) b (j f)", j=COLS)
                for n in range(parts * PIECES_PER_TILE):
                    b, part_of_map = divmod(n, parts)
                    pieces.append(
                        (
                            y_flat[:, n * PIECE : (n + 1) * PIECE],
                            rows_of_out[:, b, part_of_map * PIECE : (part_of_map + 1) * PIECE],
                        )
                    )

            stats = keep.tile([P, TILES, CHUNKS, 6], F32)
            mean_var = keep.tile([P, TILES, 2], F32)
            minus_mean_vector = keep.tile([P, TILES], F32)
            bank_sums = keep.tile([P, TILES, CHUNKS], F32)
            totals = keep.tile([P, TILES, 2], F32)
            minus_mean_scalar = keep.tile([P, TILES], F32)
            inverse_deviation = keep.tile([P, TILES], F32)
            scale = keep.tile([P, TILES], F32)
            last_shift = keep.tile([P, 1], F32)

            def statistics_on_scalar(r):
                return r > 1 and r % 2 == 1

            def multiply(r, s):
                m, y, h = column_tiles[r]
                pixels = slice(s * N_TILE, (s + 1) * N_TILE)
                bank = psum.tile([P, N_TILE], F32, tag="bank")
                for g in range(PASSES):
                    nc.tensor.matmul_mx(
                        out=bank[:],
                        lhsT=w_words[:, g, 2 * m * M_TILE : 2 * (m + 1) * M_TILE].bitcast(FP4X4),
                        lhsT_scale=w_scale_planes[:, g, m * M_TILE : (m + 1) * M_TILE],
                        rhs=x_codes[:, g, pixels].bitcast(FP8X4),
                        rhs_scale=x_scale_planes[:, g, pixels],
                        start=(g == 0),
                        stop=(g == PASSES - 1),
                    )
                y_chunk = y[:, :, s * CHUNK_COLS : (s + 1) * CHUNK_COLS, h, :]
                if statistics_on_scalar(r):
                    nc.scalar.activation(
                        out=y_chunk.rearrange("p b j i -> p j b i"),
                        in_=bank[:].rearrange("p (j b i) -> p j b i", j=CHUNK_COLS, b=MAPS),
                        func=ACT.Identity,
                        accum_out=bank_sums[:, r, s : s + 1],
                    )
                else:
                    nc.scalar.copy(
                        out=y_chunk.rearrange("p b j i -> p j b i"),
                        in_=bank[:].rearrange("p (j b i) -> p j b i", j=CHUNK_COLS, b=MAPS),
                    )
                    nc.vector.bn_stats(out=stats[:, r, s, :], in_=y_chunk)

            def begin_scale(r):
                one = slice(r, r + 1)
                if statistics_on_scalar(r):
                    y, h = column_tiles[r][1], column_tiles[r][2]
                    nc.scalar.activation(
                        out=discarded[:, 0:CHUNKS], in_=bank_sums[:, r, :], func=ACT.Identity,
                        scale=-1.0 / PIXELS, accum_out=minus_mean_scalar[:, one],
                    )
                    nc.scalar.activation(
                        out=discarded[:].rearrange("p (b j i) -> p b j i", b=MAPS, i=ROWS),
                        in_=y[:, :, :, h, :],
                        func=ACT.Square,
                        bias=minus_mean_scalar[:, one],
                        scale=1.0,
                        accum_out=totals[:, r, 1:2],
                    )
                    nc.scalar.activation(
                        out=inverse_deviation[:, one], in_=totals[:, r, 1:2],
                        func=ACT.Abs_reciprocal_sqrt, bias=eps[:, 0:1], scale=1.0 / PIXELS,
                    )
                else:
                    nc.vector.bn_aggr(
                        out=mean_var[:, r, :], in_=stats[:, r, :, :].rearrange("p s k -> p (s k)")
                    )
                    nc.vector.tensor_scalar_mul(
                        out=minus_mean_vector[:, one], in0=mean_var[:, r, 0:1], scalar1=-1.0
                    )
                    nc.scalar.activation(
                        out=inverse_deviation[:, one], in_=mean_var[:, r, 1:2],
                        func=ACT.Abs_reciprocal_sqrt, bias=eps[:, 0:1], scale=1.0,
                    )

            def finish_scale(r):
                m = column_tiles[r][0]
                nc.scalar.activation(
                    out=scale[:, r : r + 1], in_=inverse_deviation[:, r : r + 1], func=ACT.Identity,
                    scale=gain[:, m : m + 1],
                )

            def normalise(r):
                y, h = column_tiles[r][1], column_tiles[r][2]
                minus_mean = minus_mean_scalar if statistics_on_scalar(r) else minus_mean_vector
                if r == TILES - 1:
                    nc.scalar.activation(
                        out=last_shift[:], in_=minus_mean[:, r : r + 1], func=ACT.Identity,
                        scale=scale[:, r : r + 1],
                    )
                    for b in range(MAPS):
                        nc.scalar.activation(
                            out=y[:, b, :, h, :], in_=y[:, b, :, h, :], func=ACT.Identity,
                            bias=last_shift[:, 0:1], scale=scale[:, r : r + 1],
                        )
                    return
                for b in range(MAPS):
                    nc.gpsimd.tensor_scalar(
                        out=y[:, b, :, h, :],
                        in0=y[:, b, :, h, :],
                        scalar1=minus_mean[:, r : r + 1],
                        scalar2=scale[:, r : r + 1],
                        op0=ALU.add,
                        op1=ALU.mult,
                    )

            def flip_and_store(n):
                source, destination = pieces[n]
                flipped = flipped_pool.tile([P, PIECE], F32, tag="flipped", align_bytes=64)
                nc.vector.transpose(out=flipped[:], in_=source)
                nc.sync.dma_start(out=destination, in_=flipped[:])

            transpose_chunk(0)
            for s in range(CHUNKS):
                if s + 1 < CHUNKS:
                    transpose_chunk(s + 1)
                if s + 3 < CHUNKS:
                    load_x(s + 3, 2)
                quantise_chunk(s)
                multiply(0, s)

        flipped_pool = ctx.enter_context(tc.tile_pool(name="flipped", bufs=FLIPPED_BUFS))
        late = ctx.enter_context(tc.tile_pool(name="late", bufs=1))
        discarded = late.tile([P, PIXELS], BF16)

        gain_bank = psum.tile([P, P], BF16, tag="bank")
        nc.tensor.transpose(gain_bank[:], gain_rows[:], identity_bf16[:])
        gain = keep.tile([P, TILES], F32)
        nc.vector.tensor_copy(out=gain[:], in_=gain_bank[:, 0:TILES])

        for r in range(TILES):
            if r > 0:
                for s in range(CHUNKS):
                    multiply(r, s)
            begin_scale(r)
            finish_scale(r)
            normalise(r)

        for n in range(len(pieces)):
            flip_and_store(n)
